import numpy as np
import ml_dtypes


def mxq(x, axis, fmt="e4m3"):
    dtype, down = {"e4m3": (ml_dtypes.float8_e4m3fn, 7), "e5m2": (ml_dtypes.float8_e5m2, 14)}[fmt]
    v = np.moveaxis(np.asarray(x, np.float32).astype(ml_dtypes.bfloat16).astype(np.float64), axis, -1)
    blocks = v.reshape(v.shape[:-1] + (-1, 32))
    amax = np.abs(blocks).max(-1, keepdims=True)
    byte = np.maximum(np.where(amax > 0, np.frexp(amax)[1] - 1 + 127, 0) - down, 1)
    scale = np.exp2(byte - 127.0)
    codes = (blocks / scale).astype(np.float32).astype(dtype).astype(np.float64)
    return np.moveaxis((codes * scale).reshape(v.shape), -1, axis)


WIDE = False


def mx_kscale(k):
    if not WIDE:
        return np.ones(k)
    levels = np.array([10, -10, 5, -5, 0])
    if k % 512:
        return np.exp2(np.random.permutation(np.resize(levels, k // 32))).repeat(32)
    a = np.empty((k // 512, 16))
    for p in range(k // 512):
        a[p, :8] = np.random.permutation(np.resize(levels, 8))
        for g in range(8):
            far = levels[np.abs(levels - a[p, g]) >= 10]
            a[p, g + 8] = far[np.random.randint(len(far))]
    return np.exp2(a.ravel()).repeat(32)


BF16 = ml_dtypes.bfloat16


def bf(x):
    return np.asarray(x, np.float32).astype(BF16)


def f64(x):
    return np.asarray(x).astype(np.float64)


B, S, HID, NH, NOPE, ROPE, VD, KV_RANK, SW, QB = 1, 8192, 512, 2, 64, 64, 128, 512, 384, 128
QK = NOPE + ROPE


def rotate_half(x):
    h = x.shape[-1] // 2
    return np.concatenate([-x[..., h:], x[..., :h]], axis=-1)


def rope_tables():
    pos = np.arange(S, dtype=np.float64)
    inv = 1.0 / (10000.0 ** (np.arange(0, ROPE, 2, dtype=np.float64) / ROPE))
    ang = pos[:, None] * inv[None, :]
    ang = np.concatenate([ang, ang], axis=-1)
    return bf(np.broadcast_to(np.cos(ang)[None], (B, S, ROPE))), bf(np.broadcast_to(np.sin(ang)[None], (B, S, ROPE)))


def setup_inputs():
    s = mx_kscale(HID)
    cos, sin = rope_tables()
    return {"hidden_states": bf(np.random.standard_normal((B, S, HID)) * s), "cos": cos, "sin": sin,
            "Wq": bf(np.random.standard_normal((HID, NH * QK)) * 2.0 / np.sqrt(HID) / s[:, None]),
            "bq": bf(np.random.standard_normal(NH * QK) * 0.2)}


def reference(hidden_states, cos, sin, Wq, bq):
    q = ((mxq(f64(hidden_states), 2, "e4m3") @ mxq(f64(Wq), 0, "e4m3")) + f64(bq)).reshape(B, S, NH, QK).transpose(0, 2, 1, 3)
    q_nope, q_rope = q[..., :NOPE], q[..., NOPE:]
    c, si = f64(cos)[:, None], f64(sin)[:, None]
    q_rope = q_rope * c + rotate_half(q_rope) * si
    return np.concatenate([q_nope, q_rope], axis=-1)

@@ -1,0 +1,278 @@
+import concourse.mybir as mybir
+from concourse.masks import make_identity
+
+F32 = mybir.dt.float32
+BF16 = mybir.dt.bfloat16
+U32 = mybir.dt.uint32
+U8 = mybir.dt.uint8
+FP8X4 = mybir.dt.float8_e4m3fn_x4
+ADD = mybir.AluOpType.add
+SUBTRACT = mybir.AluOpType.subtract
+MULT = mybir.AluOpType.mult
+IDENTITY = mybir.ActivationFunctionType.Identity
+
+P = 128
+TOKENS = 8192
+HID = 512
+HEADS = 2
+HEAD_DIM = 128
+NOPE = 64
+ROPE = 64
+HALF = ROPE // 2
+FEATURES = HEADS * HEAD_DIM
+PACK = 4
+SLOTS = TOKENS // P
+GROUP = 4
+GROUPS = SLOTS // GROUP
+CHUNK = 8
+CHUNKS = SLOTS // CHUNK
+CHUNK_GROUPS = CHUNK // GROUP
+TABLE_SLOTS = 32
+
+FLOPS = 2 * TOKENS * HID * FEATURES
+
+
+def tile_gptossmlaattention_pb_t_kernel(tc, hidden_states, cos, sin, Wq, bq, out):
+    nc = tc.nc
+    hidden_view = hidden_states.flatten_outer_dims().rearrange("(p t) k -> p t k", t=SLOTS)
+    cos_view = cos.flatten_outer_dims().rearrange("(p t) c -> p t c", t=SLOTS)
+    sin_view = sin.flatten_outer_dims().rearrange("(p t) c -> p t c", t=SLOTS)
+    out_view = out.flatten_outer_dims().rearrange("(h p t) d -> p h t d", h=HEADS, t=SLOTS)
+
+    with tc.tile_pool(name="const", bufs=1) as const, tc.tile_pool(
+        name="resident", bufs=CHUNKS
+    ) as resident, tc.tile_pool(name="tables", bufs=SLOTS // TABLE_SLOTS) as tables, tc.tile_pool(
+        name="stage", bufs=3
+    ) as stage, tc.psum_pool(name="psum", bufs=2) as psum, tc.manual_schedule():
+        bias_row = const.tile([P, FEATURES], BF16)
+        nc.vector.memset(bias_row[:], 0.0)
+        bq_by_kind = bq.rearrange("(o h x d) -> o x h d", o=1, h=HEADS, x=2)
+        for x in range(2):
+            nc.sync.dma_start(
+                out=bias_row[0:1, x * P : (x + 1) * P].rearrange("o (h d) -> o h d", h=HEADS),
+                in_=bq_by_kind[:, x],
+            )
+
+        x_chunks = []
+        for c in range(CHUNKS):
+            x_sb = resident.tile([P, CHUNK, HID], BF16)
+            x_chunks.append(x_sb)
+
+        def load_hidden(slot0, count):
+            first = slot0 % CHUNK
+            nc.sync.dma_start(
+                out=x_chunks[slot0 // CHUNK][:, first : first + count, :],
+                in_=hidden_view[:, slot0 : slot0 + count, :],
+            )
+
+        w_raw = const.tile([P, PACK, FEATURES], BF16)
+        cos_parts = []
+        sin_parts = []
+        for c in range(CHUNKS):
+            if c == 0:
+                load_hidden(0, GROUP)
+                nc.sync.dma_start(out=w_raw[:], in_=Wq.rearrange("(p t) c -> p t c", t=PACK))
+                load_hidden(GROUP, GROUP)
+            else:
+                load_hidden(c * CHUNK, CHUNK)
+            if ((c - 1) * CHUNK) % TABLE_SLOTS == 0:
+                part = slice((c - 1) * CHUNK, (c - 1) * CHUNK + TABLE_SLOTS)
+                cos_sb = tables.tile([P, TABLE_SLOTS, ROPE], BF16)
+                nc.sync.dma_start(out=cos_sb[:], in_=cos_view[:, part, :])
+                cos_parts.append(cos_sb)
+                sin_sb = tables.tile([P, TABLE_SLOTS, ROPE], BF16)
+                nc.sync.dma_start(out=sin_sb[:], in_=sin_view[:, part, :])
+                sin_parts.append(sin_sb)
+
+        ident = const.tile([P, P], F32)
+        make_identity(nc, ident[:])
+
+        w_grouped = const.tile([P, 2, P, PACK], BF16, align_bytes=64)
+        w_by_kind = w_raw[:].rearrange("p t (h x d) -> p x h d t", h=HEADS, x=2)
+        ones = const.tile([P, P], BF16)
+        nc.vector.memset(ones[:], 1.0)
+        for x in range(2):
+            nc.vector.tensor_copy(
+                out=w_grouped[:, x].rearrange("p (h d) t -> p h d t", h=HEADS), in_=w_by_kind[:, x]
+            )
+        w_codes = const.tile([P, FEATURES], U32, align_bytes=64)
+        w_scales = const.tile([P, FEATURES], U8, align_bytes=64)
+        nc.vector.quantize_mx(
+            out=w_codes[:].bitcast(FP8X4),
+            scales=w_scales[:],
+            in_=w_grouped[:].rearrange("p x c t -> p (x c t)"),
+        )
+        stay = slice(0, P)
+        turn = slice(P, 2 * P)
+
+        setup_ps = psum.tile([P, FEATURES + ROPE], F32, tag="x_turn")
+        nc.tensor.matmul(
+            out=setup_ps[:, 0:FEATURES], lhsT=ones[:], rhs=bias_row[:], start=True, stop=True
+        )
+        nc.tensor.matmul(
+            out=setup_ps[:, FEATURES : FEATURES + ROPE],
+            lhsT=bias_row[:, turn],
+            rhs=ones[:, 0:ROPE],
+            start=True,
+            stop=True,
+        )
+        bias_stay = const.tile([P, HEADS, NOPE], F32)
+        nc.vector.tensor_copy(
+            out=bias_stay[:], in_=setup_ps[:, stay].rearrange("p (h d) -> p h d", h=HEADS)
+        )
+        bias_turn = const.tile([P, 1], F32)
+        nc.vector.tensor_copy(out=bias_turn[:], in_=setup_ps[:, FEATURES : FEATURES + 1])
+
+        grouped_of = {}
+        codes_of = {}
+        scales_of = {}
+        q_stay_of = {}
+        q_turn_t_of = {}
+        x_turn_t_of = {}
+        x_turn_of = {}
+        out_of = {}
+
+        def transpose_hidden(g):
+            x_words = x_chunks[g // CHUNK_GROUPS][:].bitcast(F32)
+            first = (g % CHUNK_GROUPS) * GROUP
+            grouped = stage.tile([P, GROUP * P * PACK], BF16, align_bytes=64)
+            grouped_words = grouped[:].bitcast(F32).rearrange("p (r u) -> p r u", u=2)
+            for pair in range(GROUP // 2):
+                x_t = psum.tile([P, 2, 2 * P], F32)
+                for i in range(2):
+                    for u in range(2):
+                        nc.tensor.transpose(
+                            x_t[:, u, i * P : (i + 1) * P],
+                            x_words[:, first + 2 * pair + i, u : 2 * P : 2],
+                            ident[:],
+                        )
+                nc.scalar.copy(
+                    out=grouped_words[:, pair * 2 * P : (pair + 1) * 2 * P, :],
+                    in_=x_t[:].rearrange("p u r -> p r u"),
+                )
+            grouped_of[g] = grouped
+
+        def quantise(g):
+            codes = stage.tile([P, GROUP * P], U32, align_bytes=64)
+            scales = stage.tile([P, GROUP * P], U8, align_bytes=64)
+            nc.vector.quantize_mx(
+                out=codes[:].bitcast(FP8X4), scales=scales[:], in_=grouped_of[g][:]
+            )
+            codes_of[g] = codes
+            scales_of[g] = scales
+
+        def multiply(g):
+            codes = codes_of[g]
+            scales = scales_of[g]
+            q_stay = psum.tile([P, GROUP, P], F32)
+            for i in range(GROUP):
+                cols = slice(i * P, (i + 1) * P)
+                nc.tensor.matmul_mx(
+                    out=q_stay[:, i, :],
+                    lhsT=codes[:, cols].bitcast(FP8X4),
+                    lhsT_scale=scales[:, cols],
+                    rhs=w_codes[:, stay].bitcast(FP8X4),
+                    rhs_scale=w_scales[:, stay],
+                    start=True,
+                    stop=True,
+                )
+            q_turn_t = psum.tile([P, GROUP * P], F32)
+            nc.tensor.matmul_mx(
+                out=q_turn_t[:],
+                lhsT=w_codes[:, turn].bitcast(FP8X4),
+                lhsT_scale=w_scales[:, turn],
+                rhs=codes[:].bitcast(FP8X4),
+                rhs_scale=scales[:],
+                start=True,
+                stop=True,
+            )
+            q_stay_of[g] = q_stay
+            q_turn_t_of[g] = q_turn_t
+
+        def add_turn_bias(g):
+            x_turn_t = stage.tile([P, GROUP * P], F32)
+            nc.scalar.activation(
+                out=x_turn_t[:], in_=q_turn_t_of[g][:], func=IDENTITY, bias=bias_turn[:], scale=1.0
+            )
+            x_turn_t_of[g] = x_turn_t
+
+        def transpose_back(g):
+            x_turn = psum.tile([P, GROUP, P], F32)
+            for i in range(GROUP):
+                nc.tensor.transpose(
+                    x_turn[:, i, :], x_turn_t_of[g][:, i * P : (i + 1) * P], ident[:]
+                )
+            x_turn_of[g] = x_turn
+
+        def out_slots(g):
+            first = (g % CHUNK_GROUPS) * GROUP
+            by_slot = out_of[g // CHUNK_GROUPS][:].rearrange("p h t d -> p t h d")
+            return by_slot[:, first : first + GROUP]
+
+        def finish_stay(g):
+            if g % CHUNK_GROUPS == 0:
+                out_sb = resident.tile([P, HEADS, CHUNK, HEAD_DIM], F32)
+                out_of[g // CHUNK_GROUPS] = out_sb
+            nc.vector.tensor_tensor(
+                out=out_slots(g)[:, :, :, 0:NOPE],
+                in0=q_stay_of[g][:].rearrange("p i (h d) -> p i h d", h=HEADS),
+                in1=bias_stay[:].unsqueeze(1).to_broadcast([P, GROUP, HEADS, NOPE]),
+                op=ADD,
+            )
+
+        def rotate(g):
+            slot0 = g * GROUP
+            in_part = slice(slot0 % TABLE_SLOTS, slot0 % TABLE_SLOTS + GROUP)
+            both_heads = [P, GROUP, HEADS, ROPE]
+            cos_g = cos_parts[slot0 // TABLE_SLOTS][:, in_part, :].unsqueeze(2).to_broadcast(both_heads)
+            sin_g = sin_parts[slot0 // TABLE_SLOTS][:, in_part, :].unsqueeze(2).to_broadcast(both_heads)
+            x_turn = x_turn_of[g][:].rearrange("p i (h d) -> p i h d", h=HEADS)
+            out_rope = out_slots(g)[:, :, :, NOPE:HEAD_DIM]
+            turned = stage.tile([P, GROUP, HEADS, ROPE], F32)
+            low = slice(0, HALF)
+            high = slice(HALF, ROPE)
+            nc.vector.tensor_tensor(out=out_rope, in0=x_turn, in1=cos_g, op=MULT)
+            nc.vector.tensor_tensor(
+                out=turned[:, :, :, low], in0=x_turn[:, :, :, high], in1=sin_g[:, :, :, low], op=MULT
+            )
+            nc.vector.tensor_tensor(
+                out=turned[:, :, :, high], in0=x_turn[:, :, :, low], in1=sin_g[:, :, :, high], op=MULT
+            )
+            nc.gpsimd.tensor_tensor(
+                out=out_rope[:, :, :, low],
+                in0=out_rope[:, :, :, low],
+                in1=turned[:, :, :, low],
+                op=SUBTRACT,
+            )
+            nc.gpsimd.tensor_tensor(
+                out=out_rope[:, :, :, high],
+                in0=out_rope[:, :, :, high],
+                in1=turned[:, :, :, high],
+                op=ADD,
+            )
+            c = g // CHUNK_GROUPS
+            first = (g % CHUNK_GROUPS) * GROUP
+            if c == CHUNKS - 1:
+                nc.sync.dma_start(
+                    out=out_view[:, :, slot0 : slot0 + GROUP, :],
+                    in_=out_of[c][:, :, first : first + GROUP, :],
+                )
+            elif first + GROUP == CHUNK:
+                nc.sync.dma_start(
+                    out=out_view[:, :, c * CHUNK : (c + 1) * CHUNK, :], in_=out_of[c][:]
+                )
+
+        for s in range(GROUPS + 4):
+            if 0 <= s - 2 < GROUPS:
+                add_turn_bias(s - 2)
+            if s < GROUPS:
+                transpose_hidden(s)
+            if 0 <= s - 3 < GROUPS:
+                transpose_back(s - 3)
+            if 0 <= s - 1 < GROUPS:
+                quantise(s - 1)
+                multiply(s - 1)
+            if 0 <= s - 2 < GROUPS:
+                finish_stay(s - 2)
+            if 0 <= s - 4:
+                rotate(s - 4)

@@ -130,6 +130,7 @@ def tile_gptossmlaattention_pb_t_kernel(tc, hidden_states, cos, sin, Wq, bq, out
         q_turn_t_of = {}
         x_turn_t_of = {}
         x_turn_of = {}
+        turned_of = {}
         out_of = {}
 
         def transpose_hidden(g):
@@ -220,24 +221,44 @@ def tile_gptossmlaattention_pb_t_kernel(tc, hidden_states, cos, sin, Wq, bq, out
                 op=ADD,
             )
 
-        def rotate(g):
+        low = slice(0, HALF)
+        high = slice(HALF, ROPE)
+
+        def tables_of(g):
             slot0 = g * GROUP
             in_part = slice(slot0 % TABLE_SLOTS, slot0 % TABLE_SLOTS + GROUP)
             both_heads = [P, GROUP, HEADS, ROPE]
-            cos_g = cos_parts[slot0 // TABLE_SLOTS][:, in_part, :].unsqueeze(2).to_broadcast(both_heads)
-            sin_g = sin_parts[slot0 // TABLE_SLOTS][:, in_part, :].unsqueeze(2).to_broadcast(both_heads)
+            return [
+                parts[slot0 // TABLE_SLOTS][:, in_part, :].unsqueeze(2).to_broadcast(both_heads)
+                for parts in (cos_parts, sin_parts)
+            ]
+
+        def start_rotation(g):
+            cos_g, sin_g = tables_of(g)
             x_turn = x_turn_of[g][:].rearrange("p i (h d) -> p i h d", h=HEADS)
-            out_rope = out_slots(g)[:, :, :, NOPE:HEAD_DIM]
             turned = stage.tile([P, GROUP, HEADS, ROPE], F32)
-            low = slice(0, HALF)
-            high = slice(HALF, ROPE)
-            nc.vector.tensor_tensor(out=out_rope, in0=x_turn, in1=cos_g, op=MULT)
+            turned_of[g] = turned
+            nc.vector.tensor_tensor(
+                out=out_slots(g)[:, :, :, NOPE:HEAD_DIM], in0=x_turn, in1=cos_g, op=MULT
+            )
             nc.vector.tensor_tensor(
                 out=turned[:, :, :, low], in0=x_turn[:, :, :, high], in1=sin_g[:, :, :, low], op=MULT
             )
+
+        def end_rotation(g):
+            cos_g, sin_g = tables_of(g)
+            x_turn = x_turn_of[g][:].rearrange("p i (h d) -> p i h d", h=HEADS)
             nc.vector.tensor_tensor(
-                out=turned[:, :, :, high], in0=x_turn[:, :, :, low], in1=sin_g[:, :, :, high], op=MULT
+                out=turned_of[g][:, :, :, high],
+                in0=x_turn[:, :, :, low],
+                in1=sin_g[:, :, :, high],
+                op=MULT,
             )
+
+        def join_and_store(g):
+            slot0 = g * GROUP
+            turned = turned_of[g]
+            out_rope = out_slots(g)[:, :, :, NOPE:HEAD_DIM]
             nc.gpsimd.tensor_tensor(
                 out=out_rope[:, :, :, low],
                 in0=out_rope[:, :, :, low],
@@ -272,7 +293,10 @@ def tile_gptossmlaattention_pb_t_kernel(tc, hidden_states, cos, sin, Wq, bq, out
             if 0 <= s - 1 < GROUPS:
                 quantise(s - 1)
                 multiply(s - 1)
+            if 0 <= s - 4:
+                end_rotation(s - 4)
+                join_and_store(s - 4)
             if 0 <= s - 2 < GROUPS:
                 finish_stay(s - 2)
-            if 0 <= s - 4:
-                rotate(s - 4)
+            if 0 <= s - 3 < GROUPS:
+                start_rotation(s - 3)

@@ -43,7 +43,7 @@ def tile_gptossmlaattention_pb_t_kernel(tc, hidden_states, cos, sin, Wq, bq, out
         name="resident", bufs=CHUNKS
     ) as resident, tc.tile_pool(name="tables", bufs=SLOTS // TABLE_SLOTS) as tables, tc.tile_pool(
         name="stage", bufs=3
-    ) as stage, tc.psum_pool(name="psum", bufs=2) as psum, tc.manual_schedule():
+    ) as stage, tc.tile_pool(name="products", bufs=GROUPS) as products, tc.psum_pool(name="psum", bufs=2) as psum, tc.manual_schedule():
         bias_row = const.tile([P, FEATURES], BF16)
         nc.vector.memset(bias_row[:], 0.0)
         bq_by_kind = bq.rearrange("(o h x d) -> o x h d", o=1, h=HEADS, x=2)
@@ -233,25 +233,23 @@ def tile_gptossmlaattention_pb_t_kernel(tc, hidden_states, cos, sin, Wq, bq, out
                 for parts in (cos_parts, sin_parts)
             ]
 
-        def start_rotation(g):
+        def multiply_by_cosines(g):
             cos_g, sin_g = tables_of(g)
             x_turn = x_turn_of[g][:].rearrange("p i (h d) -> p i h d", h=HEADS)
-            turned = stage.tile([P, GROUP, HEADS, ROPE], F32)
-            turned_of[g] = turned
             nc.vector.tensor_tensor(
                 out=out_slots(g)[:, :, :, NOPE:HEAD_DIM], in0=x_turn, in1=cos_g, op=MULT
             )
-            nc.vector.tensor_tensor(
-                out=turned[:, :, :, low], in0=x_turn[:, :, :, high], in1=sin_g[:, :, :, low], op=MULT
-            )
 
-        def end_rotation(g):
+        def multiply_by_sines(g, to, source):
+            if g not in turned_of:
+                turned = products.tile([P, GROUP, HEADS, ROPE], F32)
+                turned_of[g] = turned
             cos_g, sin_g = tables_of(g)
             x_turn = x_turn_of[g][:].rearrange("p i (h d) -> p i h d", h=HEADS)
             nc.vector.tensor_tensor(
-                out=turned_of[g][:, :, :, high],
-                in0=x_turn[:, :, :, low],
-                in1=sin_g[:, :, :, high],
+                out=turned_of[g][:, :, :, to],
+                in0=x_turn[:, :, :, source],
+                in1=sin_g[:, :, :, to],
                 op=MULT,
             )
 
@@ -284,19 +282,21 @@ def tile_gptossmlaattention_pb_t_kernel(tc, hidden_states, cos, sin, Wq, bq, out
                 )
 
         for s in range(GROUPS + 4):
+            if 0 <= s - 3 < GROUPS:
+                transpose_back(s - 3)
             if 0 <= s - 2 < GROUPS:
                 add_turn_bias(s - 2)
             if s < GROUPS:
                 transpose_hidden(s)
-            if 0 <= s - 3 < GROUPS:
-                transpose_back(s - 3)
             if 0 <= s - 1 < GROUPS:
                 quantise(s - 1)
                 multiply(s - 1)
             if 0 <= s - 4:
-                end_rotation(s - 4)
+                multiply_by_sines(s - 4, high, low)
                 join_and_store(s - 4)
+            if 0 <= s - 3 < GROUPS:
+                multiply_by_cosines(s - 3)
             if 0 <= s - 2 < GROUPS:
                 finish_stay(s - 2)
             if 0 <= s - 3 < GROUPS:
-                start_rotation(s - 3)
+                multiply_by_sines(s - 3, low, high)

@@ -23,11 +23,14 @@ FEATURES = HEADS * HEAD_DIM
 PACK = 4
 SLOTS = TOKENS // P
 GROUP = 4
-GROUPS = SLOTS // GROUP
+GROUP_SLOTS = [2, 2] + [GROUP] * 14 + [2, 2]
+GROUPS = len(GROUP_SLOTS)
+GROUP_START = [sum(GROUP_SLOTS[:g]) for g in range(GROUPS)]
 CHUNK = 8
 CHUNKS = SLOTS // CHUNK
-CHUNK_GROUPS = CHUNK // GROUP
-TABLE_SLOTS = 32
+TABLE_SLOTS = [8, 24, 32]
+TABLE_AFTER = [4, 16, 40]
+TABLE_START = [sum(TABLE_SLOTS[:n]) for n in range(len(TABLE_SLOTS))]
 
 FLOPS = 2 * TOKENS * HID * FEATURES
 
@@ -41,7 +44,7 @@ def tile_gptossmlaattention_pb_t_kernel(tc, hidden_states, cos, sin, Wq, bq, out
 
     with tc.tile_pool(name="const", bufs=1) as const, tc.tile_pool(
         name="resident", bufs=CHUNKS
-    ) as resident, tc.tile_pool(name="tables", bufs=SLOTS // TABLE_SLOTS) as tables, tc.tile_pool(
+    ) as resident, tc.tile_pool(name="tables", bufs=len(TABLE_SLOTS)) as tables, tc.tile_pool(
         name="stage", bufs=3
     ) as stage, tc.tile_pool(name="products", bufs=GROUPS) as products, tc.psum_pool(name="psum", bufs=2) as psum, tc.manual_schedule():
         bias_row = const.tile([P, FEATURES], BF16)
@@ -68,20 +71,22 @@ def tile_gptossmlaattention_pb_t_kernel(tc, hidden_states, cos, sin, Wq, bq, out
         w_raw = const.tile([P, PACK, FEATURES], BF16)
         cos_parts = []
         sin_parts = []
-        for c in range(CHUNKS):
-            if c == 0:
-                load_hidden(0, GROUP)
+        pieces = [n for g, n in enumerate(GROUP_SLOTS) if GROUP_START[g] < 2 * CHUNK]
+        pieces += [CHUNK] * (CHUNKS - 2)
+        loaded = 0
+        for slots in pieces:
+            load_hidden(loaded, slots)
+            if loaded == 0:
                 nc.sync.dma_start(out=w_raw[:], in_=Wq.rearrange("(p t) c -> p t c", t=PACK))
-                load_hidden(GROUP, GROUP)
-            else:
-                load_hidden(c * CHUNK, CHUNK)
-            if ((c - 1) * CHUNK) % TABLE_SLOTS == 0:
-                part = slice((c - 1) * CHUNK, (c - 1) * CHUNK + TABLE_SLOTS)
-                cos_sb = tables.tile([P, TABLE_SLOTS, ROPE], BF16)
-                nc.sync.dma_start(out=cos_sb[:], in_=cos_view[:, part, :])
+            loaded += slots
+            if loaded in TABLE_AFTER:
+                part = TABLE_AFTER.index(loaded)
+                rows = slice(TABLE_START[part], TABLE_START[part] + TABLE_SLOTS[part])
+                cos_sb = tables.tile([P, TABLE_SLOTS[part], ROPE], BF16)
+                nc.sync.dma_start(out=cos_sb[:], in_=cos_view[:, rows, :])
                 cos_parts.append(cos_sb)
-                sin_sb = tables.tile([P, TABLE_SLOTS, ROPE], BF16)
-                nc.sync.dma_start(out=sin_sb[:], in_=sin_view[:, part, :])
+                sin_sb = tables.tile([P, TABLE_SLOTS[part], ROPE], BF16)
+                nc.sync.dma_start(out=sin_sb[:], in_=sin_view[:, rows, :])
                 sin_parts.append(sin_sb)
 
         ident = const.tile([P, P], F32)
@@ -134,11 +139,11 @@ def tile_gptossmlaattention_pb_t_kernel(tc, hidden_states, cos, sin, Wq, bq, out
         out_of = {}
 
         def transpose_hidden(g):
-            x_words = x_chunks[g // CHUNK_GROUPS][:].bitcast(F32)
-            first = (g % CHUNK_GROUPS) * GROUP
+            chunk, first = divmod(GROUP_START[g], CHUNK)
+            x_words = x_chunks[chunk][:].bitcast(F32)
             grouped = stage.tile([P, GROUP * P * PACK], BF16, align_bytes=64)
             grouped_words = grouped[:].bitcast(F32).rearrange("p (r u) -> p r u", u=2)
-            for pair in range(GROUP // 2):
+            for pair in range(GROUP_SLOTS[g] // 2):
                 x_t = psum.tile([P, 2, 2 * P], F32)
                 for i in range(2):
                     for u in range(2):
@@ -156,8 +161,11 @@ def tile_gptossmlaattention_pb_t_kernel(tc, hidden_states, cos, sin, Wq, bq, out
         def quantise(g):
             codes = stage.tile([P, GROUP * P], U32, align_bytes=64)
             scales = stage.tile([P, GROUP * P], U8, align_bytes=64)
+            tokens = GROUP_SLOTS[g] * P
             nc.vector.quantize_mx(
-                out=codes[:].bitcast(FP8X4), scales=scales[:], in_=grouped_of[g][:]
+                out=codes[:, 0:tokens].bitcast(FP8X4),
+                scales=scales[:, 0:tokens],
+                in_=grouped_of[g][:, 0 : tokens * PACK],
             )
             codes_of[g] = codes
             scales_of[g] = scales
@@ -165,8 +173,19 @@ def tile_gptossmlaattention_pb_t_kernel(tc, hidden_states, cos, sin, Wq, bq, out
         def multiply(g):
             codes = codes_of[g]
             scales = scales_of[g]
+            q_turn_t = psum.tile([P, GROUP * P], F32)
+            tokens = GROUP_SLOTS[g] * P
+            nc.tensor.matmul_mx(
+                out=q_turn_t[:, 0:tokens],
+                lhsT=w_codes[:, turn].bitcast(FP8X4),
+                lhsT_scale=w_scales[:, turn],
+                rhs=codes[:, 0:tokens].bitcast(FP8X4),
+                rhs_scale=scales[:, 0:tokens],
+                start=True,
+                stop=True,
+            )
             q_stay = psum.tile([P, GROUP, P], F32)
-            for i in range(GROUP):
+            for i in range(GROUP_SLOTS[g]):
                 cols = slice(i * P, (i + 1) * P)
                 nc.tensor.matmul_mx(
                     out=q_stay[:, i, :],
@@ -177,126 +196,126 @@ def tile_gptossmlaattention_pb_t_kernel(tc, hidden_states, cos, sin, Wq, bq, out
                     start=True,
                     stop=True,
                 )
-            q_turn_t = psum.tile([P, GROUP * P], F32)
-            nc.tensor.matmul_mx(
-                out=q_turn_t[:],
-                lhsT=w_codes[:, turn].bitcast(FP8X4),
-                lhsT_scale=w_scales[:, turn],
-                rhs=codes[:].bitcast(FP8X4),
-                rhs_scale=scales[:],
-                start=True,
-                stop=True,
-            )
             q_stay_of[g] = q_stay
             q_turn_t_of[g] = q_turn_t
 
         def add_turn_bias(g):
             x_turn_t = stage.tile([P, GROUP * P], F32)
+            tokens = GROUP_SLOTS[g] * P
             nc.scalar.activation(
-                out=x_turn_t[:], in_=q_turn_t_of[g][:], func=IDENTITY, bias=bias_turn[:], scale=1.0
+                out=x_turn_t[:, 0:tokens],
+                in_=q_turn_t_of[g][:, 0:tokens],
+                func=IDENTITY,
+                bias=bias_turn[:],
+                scale=1.0,
             )
             x_turn_t_of[g] = x_turn_t
 
         def transpose_back(g):
             x_turn = psum.tile([P, GROUP, P], F32)
-            for i in range(GROUP):
+            for i in range(GROUP_SLOTS[g]):
                 nc.tensor.transpose(
                     x_turn[:, i, :], x_turn_t_of[g][:, i * P : (i + 1) * P], ident[:]
                 )
             x_turn_of[g] = x_turn
 
         def out_slots(g):
-            first = (g % CHUNK_GROUPS) * GROUP
-            by_slot = out_of[g // CHUNK_GROUPS][:].rearrange("p h t d -> p t h d")
-            return by_slot[:, first : first + GROUP]
+            chunk, first = divmod(GROUP_START[g], CHUNK)
+            by_slot = out_of[chunk][:].rearrange("p h t d -> p t h d")
+            return by_slot[:, first : first + GROUP_SLOTS[g]]
 
         def finish_stay(g):
-            if g % CHUNK_GROUPS == 0:
+            if GROUP_START[g] % CHUNK == 0:
                 out_sb = resident.tile([P, HEADS, CHUNK, HEAD_DIM], F32)
-                out_of[g // CHUNK_GROUPS] = out_sb
+                out_of[GROUP_START[g] // CHUNK] = out_sb
+            slots = GROUP_SLOTS[g]
+            out_stay = out_slots(g)[:, :, :, 0:NOPE]
+            sums = q_stay_of[g][:].rearrange("p i (h d) -> p i h d", h=HEADS)
+            bias = bias_stay[:].unsqueeze(1).to_broadcast([P, slots, HEADS, NOPE])
+            by_vector = slice(0, min(slots, GROUP - 1))
+            by_others = slice(GROUP - 1, slots)
             nc.vector.tensor_tensor(
-                out=out_slots(g)[:, :, :, 0:NOPE],
-                in0=q_stay_of[g][:].rearrange("p i (h d) -> p i h d", h=HEADS),
-                in1=bias_stay[:].unsqueeze(1).to_broadcast([P, GROUP, HEADS, NOPE]),
-                op=ADD,
+                out=out_stay[:, by_vector], in0=sums[:, by_vector], in1=bias[:, by_vector], op=ADD
             )
+            if slots == GROUP:
+                nc.scalar.copy(out=out_stay[:, by_others], in_=sums[:, by_others])
+                nc.gpsimd.tensor_tensor(
+                    out=out_stay[:, by_others],
+                    in0=out_stay[:, by_others],
+                    in1=bias[:, by_others],
+                    op=ADD,
+                )
 
         low = slice(0, HALF)
         high = slice(HALF, ROPE)
 
-        def tables_of(g):
-            slot0 = g * GROUP
-            in_part = slice(slot0 % TABLE_SLOTS, slot0 % TABLE_SLOTS + GROUP)
-            both_heads = [P, GROUP, HEADS, ROPE]
-            return [
-                parts[slot0 // TABLE_SLOTS][:, in_part, :].unsqueeze(2).to_broadcast(both_heads)
-                for parts in (cos_parts, sin_parts)
-            ]
+        def table_of(parts, g):
+            part = max(n for n, start in enumerate(TABLE_START) if start <= GROUP_START[g])
+            first = GROUP_START[g] - TABLE_START[part]
+            slots = GROUP_SLOTS[g]
+            table = parts[part][:, first : first + slots, :]
+            return table.unsqueeze(2).to_broadcast([P, slots, HEADS, ROPE])
+
+        def turned_back(g):
+            return x_turn_of[g][:, 0 : GROUP_SLOTS[g], :].rearrange("p i (h d) -> p i h d", h=HEADS)
 
         def multiply_by_cosines(g):
-            cos_g, sin_g = tables_of(g)
-            x_turn = x_turn_of[g][:].rearrange("p i (h d) -> p i h d", h=HEADS)
             nc.vector.tensor_tensor(
-                out=out_slots(g)[:, :, :, NOPE:HEAD_DIM], in0=x_turn, in1=cos_g, op=MULT
+                out=out_slots(g)[:, :, :, NOPE:HEAD_DIM],
+                in0=turned_back(g),
+                in1=table_of(cos_parts, g),
+                op=MULT,
             )
 
         def multiply_by_sines(g, to, source):
             if g not in turned_of:
                 turned = products.tile([P, GROUP, HEADS, ROPE], F32)
                 turned_of[g] = turned
-            cos_g, sin_g = tables_of(g)
-            x_turn = x_turn_of[g][:].rearrange("p i (h d) -> p i h d", h=HEADS)
             nc.vector.tensor_tensor(
-                out=turned_of[g][:, :, :, to],
-                in0=x_turn[:, :, :, source],
-                in1=sin_g[:, :, :, to],
+                out=turned_of[g][:, 0 : GROUP_SLOTS[g], :, to],
+                in0=turned_back(g)[:, :, :, source],
+                in1=table_of(sin_parts, g)[:, :, :, to],
                 op=MULT,
             )
 
-        def join_and_store(g):
-            slot0 = g * GROUP
-            turned = turned_of[g]
-            out_rope = out_slots(g)[:, :, :, NOPE:HEAD_DIM]
-            nc.gpsimd.tensor_tensor(
-                out=out_rope[:, :, :, low],
-                in0=out_rope[:, :, :, low],
-                in1=turned[:, :, :, low],
-                op=SUBTRACT,
+        def join(g, half, op):
+            engine = nc.vector if g == GROUPS - 1 else nc.gpsimd
+            out_half = out_slots(g)[:, :, :, NOPE:HEAD_DIM][:, :, :, half]
+            engine.tensor_tensor(
+                out=out_half,
+                in0=out_half,
+                in1=turned_of[g][:, 0 : GROUP_SLOTS[g], :, half],
+                op=op,
             )
-            nc.gpsimd.tensor_tensor(
-                out=out_rope[:, :, :, high],
-                in0=out_rope[:, :, :, high],
-                in1=turned[:, :, :, high],
-                op=ADD,
-            )
-            c = g // CHUNK_GROUPS
-            first = (g % CHUNK_GROUPS) * GROUP
-            if c == CHUNKS - 1:
-                nc.sync.dma_start(
-                    out=out_view[:, :, slot0 : slot0 + GROUP, :],
-                    in_=out_of[c][:, :, first : first + GROUP, :],
-                )
-            elif first + GROUP == CHUNK:
-                nc.sync.dma_start(
-                    out=out_view[:, :, c * CHUNK : (c + 1) * CHUNK, :], in_=out_of[c][:]
-                )
 
-        for s in range(GROUPS + 4):
-            if 0 <= s - 3 < GROUPS:
-                transpose_back(s - 3)
+        def store(g):
+            chunk, first = divmod(GROUP_START[g], CHUNK)
+            end = first + GROUP_SLOTS[g]
+            if chunk < CHUNKS - 3:
+                if end < CHUNK:
+                    return
+                first = 0
+            nc.sync.dma_start(
+                out=out_view[:, :, chunk * CHUNK + first : chunk * CHUNK + end, :],
+                in_=out_of[chunk][:, :, first:end, :],
+            )
+
+        for s in range(GROUPS + 3):
             if 0 <= s - 2 < GROUPS:
                 add_turn_bias(s - 2)
             if s < GROUPS:
                 transpose_hidden(s)
+            if 0 <= s - 2 < GROUPS:
+                transpose_back(s - 2)
             if 0 <= s - 1 < GROUPS:
                 quantise(s - 1)
                 multiply(s - 1)
-            if 0 <= s - 4:
-                multiply_by_sines(s - 4, high, low)
-                join_and_store(s - 4)
-            if 0 <= s - 3 < GROUPS:
-                multiply_by_cosines(s - 3)
+            if 0 <= s - 3:
+                multiply_by_sines(s - 3, high, low)
+                join(s - 3, low, SUBTRACT)
+                join(s - 3, high, ADD)
+                store(s - 3)
             if 0 <= s - 2 < GROUPS:
                 finish_stay(s - 2)
-            if 0 <= s - 3 < GROUPS:
-                multiply_by_sines(s - 3, low, high)
+                multiply_by_cosines(s - 2)
+                multiply_by_sines(s - 2, low, high)

@@ -224,6 +224,9 @@ def tile_gptossmlaattention_pb_t_kernel(tc, hidden_states, cos, sin, Wq, bq, out
             by_slot = out_of[chunk][:].rearrange("p h t d -> p t h d")
             return by_slot[:, first : first + GROUP_SLOTS[g]]
 
+        def others_help(g):
+            return GROUP_SLOTS[g] == GROUP and g % 2 == 1
+
         def finish_stay(g):
             if GROUP_START[g] % CHUNK == 0:
                 out_sb = resident.tile([P, HEADS, CHUNK, HEAD_DIM], F32)
@@ -232,12 +235,12 @@ def tile_gptossmlaattention_pb_t_kernel(tc, hidden_states, cos, sin, Wq, bq, out
             out_stay = out_slots(g)[:, :, :, 0:NOPE]
             sums = q_stay_of[g][:].rearrange("p i (h d) -> p i h d", h=HEADS)
             bias = bias_stay[:].unsqueeze(1).to_broadcast([P, slots, HEADS, NOPE])
-            by_vector = slice(0, min(slots, GROUP - 1))
+            by_vector = slice(0, GROUP - 1 if others_help(g) else slots)
             by_others = slice(GROUP - 1, slots)
             nc.vector.tensor_tensor(
                 out=out_stay[:, by_vector], in0=sums[:, by_vector], in1=bias[:, by_vector], op=ADD
             )
-            if slots == GROUP:
+            if others_help(g):
                 nc.scalar.copy(out=out_stay[:, by_others], in_=sums[:, by_others])
                 nc.gpsimd.tensor_tensor(
                     out=out_stay[:, by_others],
@@ -278,17 +281,18 @@ def tile_gptossmlaattention_pb_t_kernel(tc, hidden_states, cos, sin, Wq, bq, out
                 op=MULT,
             )
 
-        def join(g, half, op):
-            engine = nc.vector if g == GROUPS - 1 else nc.gpsimd
-            out_half = out_slots(g)[:, :, :, NOPE:HEAD_DIM][:, :, :, half]
-            engine.tensor_tensor(
-                out=out_half,
-                in0=out_half,
-                in1=turned_of[g][:, 0 : GROUP_SLOTS[g], :, half],
-                op=op,
-            )
+        def joined_by_vector(g):
+            return g >= GROUPS - 3
 
-        def store(g):
+        def join_and_store(g, engine):
+            for half, op in ((low, SUBTRACT), (high, ADD)):
+                out_half = out_slots(g)[:, :, :, NOPE:HEAD_DIM][:, :, :, half]
+                engine.tensor_tensor(
+                    out=out_half,
+                    in0=out_half,
+                    in1=turned_of[g][:, 0 : GROUP_SLOTS[g], :, half],
+                    op=op,
+                )
             chunk, first = divmod(GROUP_START[g], CHUNK)
             end = first + GROUP_SLOTS[g]
             if chunk < CHUNKS - 3:
@@ -312,10 +316,11 @@ def tile_gptossmlaattention_pb_t_kernel(tc, hidden_states, cos, sin, Wq, bq, out
                 multiply(s - 1)
             if 0 <= s - 3:
                 multiply_by_sines(s - 3, high, low)
-                join(s - 3, low, SUBTRACT)
-                join(s - 3, high, ADD)
-                store(s - 3)
+                if not joined_by_vector(s - 3):
+                    join_and_store(s - 3, nc.gpsimd)
             if 0 <= s - 2 < GROUPS:
                 finish_stay(s - 2)
                 multiply_by_cosines(s - 2)
                 multiply_by_sines(s - 2, low, high)
+            if 0 <= s - 3 and joined_by_vector(s - 3):
+                join_and_store(s - 3, nc.vector)

import concourse.mybir as mybir
from concourse.masks import make_identity

F32 = mybir.dt.float32
BF16 = mybir.dt.bfloat16
U32 = mybir.dt.uint32
U8 = mybir.dt.uint8
FP8X4 = mybir.dt.float8_e4m3fn_x4
ADD = mybir.AluOpType.add
SUBTRACT = mybir.AluOpType.subtract
MULT = mybir.AluOpType.mult
IDENTITY = mybir.ActivationFunctionType.Identity

P = 128
TOKENS = 8192
HID = 512
HEADS = 2
HEAD_DIM = 128
NOPE = 64
ROPE = 64
HALF = ROPE // 2
FEATURES = HEADS * HEAD_DIM
PACK = 4
SLOTS = TOKENS // P
GROUP = 4
GROUP_SLOTS = [2, 2] + [GROUP] * 14 + [2, 2]
GROUPS = len(GROUP_SLOTS)
GROUP_START = [sum(GROUP_SLOTS[:g]) for g in range(GROUPS)]
CHUNK = 8
CHUNKS = SLOTS // CHUNK
TABLE_SLOTS = [8, 24, 32]
TABLE_AFTER = [4, 16, 40]
TABLE_START = [sum(TABLE_SLOTS[:n]) for n in range(len(TABLE_SLOTS))]

FLOPS = 2 * TOKENS * HID * FEATURES


def tile_gptossmlaattention_pb_t_kernel(tc, hidden_states, cos, sin, Wq, bq, out):
    nc = tc.nc
    hidden_view = hidden_states.flatten_outer_dims().rearrange("(p t) k -> p t k", t=SLOTS)
    cos_view = cos.flatten_outer_dims().rearrange("(p t) c -> p t c", t=SLOTS)
    sin_view = sin.flatten_outer_dims().rearrange("(p t) c -> p t c", t=SLOTS)
    out_view = out.flatten_outer_dims().rearrange("(h p t) d -> p h t d", h=HEADS, t=SLOTS)

    with tc.tile_pool(name="const", bufs=1) as const, tc.tile_pool(
        name="resident", bufs=CHUNKS
    ) as resident, tc.tile_pool(name="tables", bufs=len(TABLE_SLOTS)) as tables, tc.tile_pool(
        name="stage", bufs=3
    ) as stage, tc.tile_pool(name="products", bufs=GROUPS) as products, tc.psum_pool(name="psum", bufs=2) as psum, tc.manual_schedule():
        bias_row = const.tile([P, FEATURES], BF16)
        nc.vector.memset(bias_row[:], 0.0)
        bq_by_kind = bq.rearrange("(o h x d) -> o x h d", o=1, h=HEADS, x=2)
        for x in range(2):
            nc.sync.dma_start(
                out=bias_row[0:1, x * P : (x + 1) * P].rearrange("o (h d) -> o h d", h=HEADS),
                in_=bq_by_kind[:, x],
            )

        x_chunks = []
        for c in range(CHUNKS):
            x_sb = resident.tile([P, CHUNK, HID], BF16)
            x_chunks.append(x_sb)

        def load_hidden(slot0, count):
            first = slot0 % CHUNK
            nc.sync.dma_start(
                out=x_chunks[slot0 // CHUNK][:, first : first + count, :],
                in_=hidden_view[:, slot0 : slot0 + count, :],
            )

        w_raw = const.tile([P, PACK, FEATURES], BF16)
        cos_parts = []
        sin_parts = []
        pieces = [n for g, n in enumerate(GROUP_SLOTS) if GROUP_START[g] < 2 * CHUNK]
        pieces += [CHUNK] * (CHUNKS - 2)
        loaded = 0
        for slots in pieces:
            load_hidden(loaded, slots)
            if loaded == 0:
                nc.sync.dma_start(out=w_raw[:], in_=Wq.rearrange("(p t) c -> p t c", t=PACK))
            loaded += slots
            if loaded in TABLE_AFTER:
                part = TABLE_AFTER.index(loaded)
                rows = slice(TABLE_START[part], TABLE_START[part] + TABLE_SLOTS[part])
                cos_sb = tables.tile([P, TABLE_SLOTS[part], ROPE], BF16)
                nc.sync.dma_start(out=cos_sb[:], in_=cos_view[:, rows, :])
                cos_parts.append(cos_sb)
                sin_sb = tables.tile([P, TABLE_SLOTS[part], ROPE], BF16)
                nc.sync.dma_start(out=sin_sb[:], in_=sin_view[:, rows, :])
                sin_parts.append(sin_sb)

        ident = const.tile([P, P], F32)
        make_identity(nc, ident[:])

        w_grouped = const.tile([P, 2, P, PACK], BF16, align_bytes=64)
        w_by_kind = w_raw[:].rearrange("p t (h x d) -> p x h d t", h=HEADS, x=2)
        ones = const.tile([P, P], BF16)
        nc.vector.memset(ones[:], 1.0)
        for x in range(2):
            nc.vector.tensor_copy(
                out=w_grouped[:, x].rearrange("p (h d) t -> p h d t", h=HEADS), in_=w_by_kind[:, x]
            )
        w_codes = const.tile([P, FEATURES], U32, align_bytes=64)
        w_scales = const.tile([P, FEATURES], U8, align_bytes=64)
        nc.vector.quantize_mx(
            out=w_codes[:].bitcast(FP8X4),
            scales=w_scales[:],
            in_=w_grouped[:].rearrange("p x c t -> p (x c t)"),
        )
        stay = slice(0, P)
        turn = slice(P, 2 * P)

        setup_ps = psum.tile([P, FEATURES + ROPE], F32, tag="x_turn")
        nc.tensor.matmul(
            out=setup_ps[:, 0:FEATURES], lhsT=ones[:], rhs=bias_row[:], start=True, stop=True
        )
        nc.tensor.matmul(
            out=setup_ps[:, FEATURES : FEATURES + ROPE],
            lhsT=bias_row[:, turn],
            rhs=ones[:, 0:ROPE],
            start=True,
            stop=True,
        )
        bias_stay = const.tile([P, HEADS, NOPE], F32)
        nc.vector.tensor_copy(
            out=bias_stay[:], in_=setup_ps[:, stay].rearrange("p (h d) -> p h d", h=HEADS)
        )
        bias_turn = const.tile([P, 1], F32)
        nc.vector.tensor_copy(out=bias_turn[:], in_=setup_ps[:, FEATURES : FEATURES + 1])

        grouped_of = {}
        codes_of = {}
        scales_of = {}
        q_stay_of = {}
        q_turn_t_of = {}
        x_turn_t_of = {}
        x_turn_of = {}
        turned_of = {}
        out_of = {}

        def transpose_hidden(g):
            chunk, first = divmod(GROUP_START[g], CHUNK)
            x_words = x_chunks[chunk][:].bitcast(F32)
            grouped = stage.tile([P, GROUP * P * PACK], BF16, align_bytes=64)
            grouped_words = grouped[:].bitcast(F32).rearrange("p (r u) -> p r u", u=2)
            for pair in range(GROUP_SLOTS[g] // 2):
                x_t = psum.tile([P, 2, 2 * P], F32)
                for i in range(2):
                    for u in range(2):
                        nc.tensor.transpose(
                            x_t[:, u, i * P : (i + 1) * P],
                            x_words[:, first + 2 * pair + i, u : 2 * P : 2],
                            ident[:],
                        )
                nc.scalar.copy(
                    out=grouped_words[:, pair * 2 * P : (pair + 1) * 2 * P, :],
                    in_=x_t[:].rearrange("p u r -> p r u"),
                )
            grouped_of[g] = grouped

        def quantise(g):
            codes = stage.tile([P, GROUP * P], U32, align_bytes=64)
            scales = stage.tile([P, GROUP * P], U8, align_bytes=64)
            tokens = GROUP_SLOTS[g] * P
            nc.vector.quantize_mx(
                out=codes[:, 0:tokens].bitcast(FP8X4),
                scales=scales[:, 0:tokens],
                in_=grouped_of[g][:, 0 : tokens * PACK],
            )
            codes_of[g] = codes
            scales_of[g] = scales

        def multiply(g):
            codes = codes_of[g]
            scales = scales_of[g]
            q_turn_t = psum.tile([P, GROUP * P], F32)
            tokens = GROUP_SLOTS[g] * P
            nc.tensor.matmul_mx(
                out=q_turn_t[:, 0:tokens],
                lhsT=w_codes[:, turn].bitcast(FP8X4),
                lhsT_scale=w_scales[:, turn],
                rhs=codes[:, 0:tokens].bitcast(FP8X4),
                rhs_scale=scales[:, 0:tokens],
                start=True,
                stop=True,
            )
            q_stay = psum.tile([P, GROUP, P], F32)
            for i in range(GROUP_SLOTS[g]):
                cols = slice(i * P, (i + 1) * P)
                nc.tensor.matmul_mx(
                    out=q_stay[:, i, :],
                    lhsT=codes[:, cols].bitcast(FP8X4),
                    lhsT_scale=scales[:, cols],
                    rhs=w_codes[:, stay].bitcast(FP8X4),
                    rhs_scale=w_scales[:, stay],
                    start=True,
                    stop=True,
                )
            q_stay_of[g] = q_stay
            q_turn_t_of[g] = q_turn_t

        def add_turn_bias(g):
            x_turn_t = stage.tile([P, GROUP * P], F32)
            tokens = GROUP_SLOTS[g] * P
            nc.scalar.activation(
                out=x_turn_t[:, 0:tokens],
                in_=q_turn_t_of[g][:, 0:tokens],
                func=IDENTITY,
                bias=bias_turn[:],
                scale=1.0,
            )
            x_turn_t_of[g] = x_turn_t

        def transpose_back(g):
            x_turn = psum.tile([P, GROUP, P], F32)
            for i in range(GROUP_SLOTS[g]):
                nc.tensor.transpose(
                    x_turn[:, i, :], x_turn_t_of[g][:, i * P : (i + 1) * P], ident[:]
                )
            x_turn_of[g] = x_turn

        def out_slots(g):
            chunk, first = divmod(GROUP_START[g], CHUNK)
            by_slot = out_of[chunk][:].rearrange("p h t d -> p t h d")
            return by_slot[:, first : first + GROUP_SLOTS[g]]

        def others_help(g):
            return GROUP_SLOTS[g] == GROUP and g % 2 == 1

        def finish_stay(g):
            if GROUP_START[g] % CHUNK == 0:
                out_sb = resident.tile([P, HEADS, CHUNK, HEAD_DIM], F32)
                out_of[GROUP_START[g] // CHUNK] = out_sb
            slots = GROUP_SLOTS[g]
            out_stay = out_slots(g)[:, :, :, 0:NOPE]
            sums = q_stay_of[g][:].rearrange("p i (h d) -> p i h d", h=HEADS)
            bias = bias_stay[:].unsqueeze(1).to_broadcast([P, slots, HEADS, NOPE])
            by_vector = slice(0, GROUP - 1 if others_help(g) else slots)
            by_others = slice(GROUP - 1, slots)
            nc.vector.tensor_tensor(
                out=out_stay[:, by_vector], in0=sums[:, by_vector], in1=bias[:, by_vector], op=ADD
            )
            if others_help(g):
                nc.scalar.copy(out=out_stay[:, by_others], in_=sums[:, by_others])
                nc.gpsimd.tensor_tensor(
                    out=out_stay[:, by_others],
                    in0=out_stay[:, by_others],
                    in1=bias[:, by_others],
                    op=ADD,
                )

        low = slice(0, HALF)
        high = slice(HALF, ROPE)

        def table_of(parts, g):
            part = max(n for n, start in enumerate(TABLE_START) if start <= GROUP_START[g])
            first = GROUP_START[g] - TABLE_START[part]
            slots = GROUP_SLOTS[g]
            table = parts[part][:, first : first + slots, :]
            return table.unsqueeze(2).to_broadcast([P, slots, HEADS, ROPE])

        def turned_back(g):
            return x_turn_of[g][:, 0 : GROUP_SLOTS[g], :].rearrange("p i (h d) -> p i h d", h=HEADS)

        def multiply_by_cosines(g):
            nc.vector.tensor_tensor(
                out=out_slots(g)[:, :, :, NOPE:HEAD_DIM],
                in0=turned_back(g),
                in1=table_of(cos_parts, g),
                op=MULT,
            )

        def multiply_by_sines(g, to, source):
            if g not in turned_of:
                turned = products.tile([P, GROUP, HEADS, ROPE], F32)
                turned_of[g] = turned
            nc.vector.tensor_tensor(
                out=turned_of[g][:, 0 : GROUP_SLOTS[g], :, to],
                in0=turned_back(g)[:, :, :, source],
                in1=table_of(sin_parts, g)[:, :, :, to],
                op=MULT,
            )

        def joined_by_vector(g):
            return g >= GROUPS - 3

        def join_and_store(g, engine):
            for half, op in ((low, SUBTRACT), (high, ADD)):
                out_half = out_slots(g)[:, :, :, NOPE:HEAD_DIM][:, :, :, half]
                engine.tensor_tensor(
                    out=out_half,
                    in0=out_half,
                    in1=turned_of[g][:, 0 : GROUP_SLOTS[g], :, half],
                    op=op,
                )
            chunk, first = divmod(GROUP_START[g], CHUNK)
            end = first + GROUP_SLOTS[g]
            if chunk < CHUNKS - 3:
                if end < CHUNK:
                    return
                first = 0
            nc.sync.dma_start(
                out=out_view[:, :, chunk * CHUNK + first : chunk * CHUNK + end, :],
                in_=out_of[chunk][:, :, first:end, :],
            )

        for s in range(GROUPS + 3):
            if 0 <= s - 2 < GROUPS:
                add_turn_bias(s - 2)
            if s < GROUPS:
                transpose_hidden(s)
            if 0 <= s - 2 < GROUPS:
                transpose_back(s - 2)
            if 0 <= s - 1 < GROUPS:
                quantise(s - 1)
                multiply(s - 1)
            if 0 <= s - 3:
                multiply_by_sines(s - 3, high, low)
                if not joined_by_vector(s - 3):
                    join_and_store(s - 3, nc.gpsimd)
            if 0 <= s - 2 < GROUPS:
                finish_stay(s - 2)
                multiply_by_cosines(s - 2)
                multiply_by_sines(s - 2, low, high)
            if 0 <= s - 3 and joined_by_vector(s - 3):
                join_and_store(s - 3, nc.vector)
